import numpy as np
import ml_dtypes


def mxq(x, axis, fmt="e4m3"):
    dtype, down = {"e4m3": (ml_dtypes.float8_e4m3fn, 7), "e5m2": (ml_dtypes.float8_e5m2, 14)}[fmt]
    v = np.moveaxis(np.asarray(x, np.float32).astype(ml_dtypes.bfloat16).astype(np.float64), axis, -1)
    blocks = v.reshape(v.shape[:-1] + (-1, 32))
    amax = np.abs(blocks).max(-1, keepdims=True)
    byte = np.maximum(np.where(amax > 0, np.frexp(amax)[1] - 1 + 127, 0) - down, 1)
    scale = np.exp2(byte - 127.0)
    codes = (blocks / scale).astype(np.float32).astype(dtype).astype(np.float64)
    return np.moveaxis((codes * scale).reshape(v.shape), -1, axis)


WIDE = False


def mx_kscale(k):
    if not WIDE:
        return np.ones(k)
    levels = np.array([10, -10, 5, -5, 0])
    if k % 512:
        return np.exp2(np.random.permutation(np.resize(levels, k // 32))).repeat(32)
    a = np.empty((k // 512, 16))
    for p in range(k // 512):
        a[p, :8] = np.random.permutation(np.resize(levels, 8))
        for g in range(8):
            far = levels[np.abs(levels - a[p, g]) >= 10]
            a[p, g + 8] = far[np.random.randint(len(far))]
    return np.exp2(a.ravel()).repeat(32)


BF16 = ml_dtypes.bfloat16


def bf(x):
    return np.asarray(x, np.float32).astype(BF16)


def f64(x):
    return np.asarray(x).astype(np.float64)


B, T, C, NH, NC = 1, 4096, 2048, 16, 2
HS = C // NH
N = T // NC


def setup_inputs():
    s = mx_kscale(C)
    t = mx_kscale(T)
    return {"x": bf(np.random.standard_normal((B, T, C)) * s * t[:, None]),
            "Wk": bf(np.random.standard_normal((C, C)) / np.sqrt(C) / s),
            "pk_W": bf(np.random.standard_normal((NC, N, N)) / np.sqrt(N) / t.reshape(NC, 1, N)),
            "pk_b": bf(np.random.standard_normal((NC, N)) * 0.3)}


def reference(x, Wk, pk_W, pk_b):
    kh = mxq(f64(x), 2, "e4m3") @ mxq(f64(Wk), 1, "e4m3").T
    kh = kh.reshape(B, T, NH, HS).transpose(0, 2, 1, 3).reshape(B, NH, NC, N, HS)
    out = (mxq(f64(pk_W), 2, "e4m3") @ mxq(kh, 3, "e4m3")) + f64(pk_b)[:, :, None]
    return out.reshape(B, NH, T, HS)

@@ -1,0 +1,202 @@
+from contextlib import ExitStack
+
+import concourse.mybir as mybir
+from concourse.masks import make_identity
+
+FLOPS = 2 * 4096 * 2048 * 2048 * 2
+
+F32 = mybir.dt.float32
+BF16 = mybir.dt.bfloat16
+U32 = mybir.dt.uint32
+U8 = mybir.dt.uint8
+FP8X4 = mybir.dt.float8_e4m3fn_x4
+ACT = mybir.ActivationFunctionType
+ALU = mybir.AluOpType
+
+P = 128
+RAW_BUFS = 6
+
+
+def tile_causalselfattention_pa_l_kernel(tc, x, Wk, pk_W, pk_b, out):
+    nc = tc.nc
+    xf = x.flatten_outer_dims()
+    pf = pk_W.flatten_outer_dims()
+
+    with ExitStack() as ctx:
+        const = ctx.enter_context(tc.tile_pool(name="const", bufs=1))
+        keep = ctx.enter_context(tc.tile_pool(name="keep", bufs=1))
+        rawp = ctx.enter_context(tc.tile_pool(name="rawp", bufs=RAW_BUFS))
+        grpp = ctx.enter_context(tc.tile_pool(name="grpp", bufs=4))
+        stap = ctx.enter_context(tc.tile_pool(name="stap", bufs=2))
+        khbp = ctx.enter_context(tc.tile_pool(name="khbp", bufs=3))
+        khgp = ctx.enter_context(tc.tile_pool(name="khgp", bufs=3))
+        ostp = ctx.enter_context(tc.tile_pool(name="ostp", bufs=3))
+        accp = ctx.enter_context(tc.psum_pool(name="accp", bufs=4))
+        trpp = ctx.enter_context(tc.psum_pool(name="trpp", bufs=4))
+
+        ident = const.tile([P, P], F32, name="ident")
+        make_identity(nc, ident[:])
+        warm_in = const.tile([P, 8], F32, name="warm_in")
+        warm_out = const.tile([P, 8], F32, name="warm_out")
+        bias_raw = const.tile([P, 8, 4], BF16, name="bias_raw")
+        bias_f32 = const.tile([P, 32], F32, name="bias_f32")
+
+        moving = {}
+        for j in range(4):
+            moving[("w", j)] = (
+                keep.tile([P, 4, 512], U32, name="wkc%d" % j, align_bytes=64),
+                keep.tile([P, 4, 512], U8, name="wks%d" % j, align_bytes=64),
+            )
+            moving[("k", j)] = (
+                keep.tile([P, 4, 512], U32, name="khc%d" % j, align_bytes=64),
+                keep.tile([P, 4, 512], U8, name="khs%d" % j, align_bytes=64),
+            )
+
+        halves = [("s", 0, 0), ("w", 0, 0), ("s", 0, 1), ("w", 0, 1)]
+        halves.extend([("w", j, h) for j in range(1, 4) for h in range(2)])
+        halves.extend([("s", s, h) for s in range(1, 16) for h in range(2)])
+
+        raws = {}
+        stationary = {}
+
+        def source(kind, idx, h):
+            cols = slice(1024 * h, 1024 * (h + 1))
+            if kind == "w":
+                return Wk[512 * idx : 512 * (idx + 1), cols].rearrange("(a p) k -> p a k", p=P)
+            src = xf if (idx // 4) % 2 == 0 else pf
+            r0 = 2048 * (idx // 8) + 512 * (idx % 4)
+            return src[r0 : r0 + 512, cols].rearrange("(p a) k -> p a k", a=4)
+
+        def load(k):
+            kind, idx, h = halves[k]
+            raw = rawp.tile([P, 4, 1024], BF16, name="raw")
+            nc.sync.dma_start(out=raw[:], in_=source(kind, idx, h))
+            raws[k] = raw
+
+        def prep(k):
+            kind, idx, h = halves[k]
+            if kind == "w":
+                codes, scales = moving[("w", idx)]
+            else:
+                if h == 0:
+                    stationary[idx] = (
+                        stap.tile([P, 4, 512], U32, name="stc", align_bytes=64),
+                        stap.tile([P, 4, 512], U8, name="sts", align_bytes=64),
+                    )
+                codes, scales = stationary[idx]
+            words = raws[k][:].bitcast(F32)
+            grouped = []
+            for gl in range(2):
+                grp = grpp.tile([P, 2048], BF16, name="grp", align_bytes=64)
+                grouped.append(grp)
+                gw = grp[:].bitcast(F32)
+                for half in range(2):
+                    tp = trpp.tile([P, 512], F32, name="tp")
+                    for a2 in range(2):
+                        for u in range(2):
+                            q = 2 * a2 + u
+                            nc.tensor.transpose(
+                                tp[:, 128 * q : 128 * (q + 1)],
+                                words[:, 2 * half + a2, 256 * gl + u : 256 * (gl + 1) : 2],
+                                ident[:],
+                            )
+                    dst = gw[:, 512 * half : 512 * (half + 1)].rearrange("p (a r u) -> p a r u", a=2, u=2)
+                    srcv = tp[:].rearrange("p (a u r) -> p a r u", a=2, u=2)
+                    if half == 0:
+                        nc.vector.tensor_copy(out=dst, in_=srcv)
+                    else:
+                        nc.scalar.copy(out=dst, in_=srcv)
+            for gl in range(2):
+                g = 2 * h + gl
+                nc.vector.quantize_mx(
+                    out=codes[:, g, :].bitcast(FP8X4),
+                    scales=scales[:, g, :],
+                    in_=grouped[gl][:],
+                )
+            if k + RAW_BUFS < len(halves):
+                load(k + RAW_BUFS)
+
+        def unit(s, j):
+            first_stage = (s // 4) % 2 == 0
+            stc, sts = stationary[s]
+            mvc, mvs = moving[("w" if first_stage else "k", j)]
+            if first_stage:
+                khb = khbp.tile([P, 4, 512], BF16, name="khb")
+            else:
+                ost = ostp.tile([P, 4, 4, 128], F32, name="ost")
+            for t in range(4):
+                acc = accp.tile([P, 512], F32, name="acc")
+                cols = slice(128 * t, 128 * (t + 1))
+                for g in range(4):
+                    nc.tensor.matmul_mx(
+                        out=acc[:],
+                        lhsT=stc[:, g, cols].bitcast(FP8X4),
+                        lhsT_scale=sts[:, g, cols],
+                        rhs=mvc[:, g, :].bitcast(FP8X4),
+                        rhs_scale=mvs[:, g, :],
+                        start=(g == 0),
+                        stop=(g == 3),
+                    )
+                if first_stage:
+                    nc.scalar.copy(out=khb[:, t, :], in_=acc[:])
+                else:
+                    col = 4 * (4 * (s // 8) + s % 4) + t
+                    accv = acc[:].rearrange("p (h d) -> p h d", h=4)
+                    if t % 2 == 0:
+                        nc.scalar.activation(
+                            out=ost[:, :, t, :], in_=accv, func=ACT.Identity,
+                            bias=bias_f32[:, col : col + 1], scale=1.0,
+                        )
+                    else:
+                        nc.vector.tensor_scalar(
+                            out=ost[:, :, t, :], in0=accv,
+                            scalar1=bias_f32[:, col : col + 1], scalar2=None, op0=ALU.add,
+                        )
+            if first_stage:
+                khg = khgp.tile([P, 512, 4], BF16, name="khg", align_bytes=64)
+                nc.vector.tensor_copy(out=khg[:], in_=khb[:].rearrange("p t c -> p c t"))
+                khc, khs = moving[("k", j)]
+                nc.vector.quantize_mx(
+                    out=khc[:, s % 4, :].bitcast(FP8X4),
+                    scales=khs[:, s % 4, :],
+                    in_=khg[:].rearrange("p c t -> p (c t)"),
+                )
+            else:
+                r0 = 2048 * (s // 8) + 512 * (s % 4)
+                nc.sync.dma_start(
+                    out=out[0, 4 * j : 4 * (j + 1), r0 : r0 + 512, :].rearrange("h (p a) d -> p h (a d)", a=4),
+                    in_=ost[:].rearrange("p h a d -> p h (a d)"),
+                )
+
+        ctx.enter_context(tc.manual_schedule())
+
+        nc.vector.memset(warm_in[:], 0.0)
+        nc.scalar.activation(out=warm_out[:], in_=warm_in[:], func=ACT.Identity)
+        for k in range(RAW_BUFS):
+            load(k)
+
+        for k in range(5):
+            prep(k)
+        unit(0, 0)
+        prep(5)
+        prep(6)
+        unit(0, 1)
+        prep(7)
+        prep(8)
+        unit(0, 2)
+        prep(9)
+        prep(10)
+        prep(11)
+        unit(0, 3)
+        nc.sync.dma_start(out=bias_raw[:], in_=pk_b.rearrange("c (b p a) -> p (c b) a", p=P, a=4))
+        for s in range(1, 16):
+            if s < 15:
+                prep(10 + 2 * s)
+            unit(s, 0)
+            unit(s, 1)
+            if s < 15:
+                prep(11 + 2 * s)
+            unit(s, 2)
+            unit(s, 3)
+            if s == 1:
+                nc.vector.tensor_copy(out=bias_f32[:], in_=bias_raw[:].rearrange("p b a -> p (b a)"))

@@ -14,7 +14,7 @@ ACT = mybir.ActivationFunctionType
 ALU = mybir.AluOpType
 
 P = 128
-RAW_BUFS = 6
+RAW_BUFS = 5
 
 
 def tile_causalselfattention_pa_l_kernel(tc, x, Wk, pk_W, pk_b, out):
@@ -26,6 +26,7 @@ def tile_causalselfattention_pa_l_kernel(tc, x, Wk, pk_W, pk_b, out):
         const = ctx.enter_context(tc.tile_pool(name="const", bufs=1))
         keep = ctx.enter_context(tc.tile_pool(name="keep", bufs=1))
         rawp = ctx.enter_context(tc.tile_pool(name="rawp", bufs=RAW_BUFS))
+        srtp = ctx.enter_context(tc.tile_pool(name="srtp", bufs=2))
         grpp = ctx.enter_context(tc.tile_pool(name="grpp", bufs=4))
         stap = ctx.enter_context(tc.tile_pool(name="stap", bufs=2))
         khbp = ctx.enter_context(tc.tile_pool(name="khbp", bufs=3))
@@ -57,7 +58,9 @@ def tile_causalselfattention_pa_l_kernel(tc, x, Wk, pk_W, pk_b, out):
         halves.extend([("s", s, h) for s in range(1, 16) for h in range(2)])
 
         raws = {}
+        srts = {}
         stationary = {}
+        pending_q = [None]
 
         def source(kind, idx, h):
             cols = slice(1024 * h, 1024 * (h + 1))
@@ -73,8 +76,20 @@ def tile_causalselfattention_pa_l_kernel(tc, x, Wk, pk_W, pk_b, out):
             nc.sync.dma_start(out=raw[:], in_=source(kind, idx, h))
             raws[k] = raw
 
+        def sort(k):
+            srt = srtp.tile([P, 8, 2, 128], F32, name="srt")
+            nc.vector.tensor_copy(
+                out=srt[:],
+                in_=raws[k][:].bitcast(F32).rearrange("p a (g i u) -> p (a g) u i", g=2, u=2),
+            )
+            srts[k] = srt
+            if k + RAW_BUFS < len(halves):
+                load(k + RAW_BUFS)
+
         def prep(k):
             kind, idx, h = halves[k]
+            if k + 1 < len(halves):
+                sort(k + 1)
             if kind == "w":
                 codes, scales = moving[("w", idx)]
             else:
@@ -84,7 +99,7 @@ def tile_causalselfattention_pa_l_kernel(tc, x, Wk, pk_W, pk_b, out):
                         stap.tile([P, 4, 512], U8, name="sts", align_bytes=64),
                     )
                 codes, scales = stationary[idx]
-            words = raws[k][:].bitcast(F32)
+            srt = srts[k]
             grouped = []
             for gl in range(2):
                 grp = grpp.tile([P, 2048], BF16, name="grp", align_bytes=64)
@@ -97,15 +112,12 @@ def tile_causalselfattention_pa_l_kernel(tc, x, Wk, pk_W, pk_b, out):
                             q = 2 * a2 + u
                             nc.tensor.transpose(
                                 tp[:, 128 * q : 128 * (q + 1)],
-                                words[:, 2 * half + a2, 256 * gl + u : 256 * (gl + 1) : 2],
+                                srt[:, 2 * (2 * half + a2) + gl, u, :],
                                 ident[:],
                             )
                     dst = gw[:, 512 * half : 512 * (half + 1)].rearrange("p (a r u) -> p a r u", a=2, u=2)
                     srcv = tp[:].rearrange("p (a u r) -> p a r u", a=2, u=2)
-                    if half == 0:
-                        nc.vector.tensor_copy(out=dst, in_=srcv)
-                    else:
-                        nc.scalar.copy(out=dst, in_=srcv)
+                    nc.scalar.copy(out=dst, in_=srcv)
             for gl in range(2):
                 g = 2 * h + gl
                 nc.vector.quantize_mx(
@@ -113,8 +125,17 @@ def tile_causalselfattention_pa_l_kernel(tc, x, Wk, pk_W, pk_b, out):
                     scales=scales[:, g, :],
                     in_=grouped[gl][:],
                 )
-            if k + RAW_BUFS < len(halves):
-                load(k + RAW_BUFS)
+
+        def flush_q():
+            if pending_q[0] is not None:
+                khg, j, g = pending_q[0]
+                khc, khs = moving[("k", j)]
+                nc.vector.quantize_mx(
+                    out=khc[:, g, :].bitcast(FP8X4),
+                    scales=khs[:, g, :],
+                    in_=khg[:].rearrange("p c t -> p (c t)"),
+                )
+            pending_q[0] = None
 
         def unit(s, j):
             first_stage = (s // 4) % 2 == 0
@@ -155,12 +176,10 @@ def tile_causalselfattention_pa_l_kernel(tc, x, Wk, pk_W, pk_b, out):
             if first_stage:
                 khg = khgp.tile([P, 512, 4], BF16, name="khg", align_bytes=64)
                 nc.vector.tensor_copy(out=khg[:], in_=khb[:].rearrange("p t c -> p c t"))
-                khc, khs = moving[("k", j)]
-                nc.vector.quantize_mx(
-                    out=khc[:, s % 4, :].bitcast(FP8X4),
-                    scales=khs[:, s % 4, :],
-                    in_=khg[:].rearrange("p c t -> p (c t)"),
-                )
+                flush_q()
+                pending_q[0] = (khg, j, s % 4)
+                if s % 4 == 3 and j == 3:
+                    flush_q()
             else:
                 r0 = 2048 * (s // 8) + 512 * (s % 4)
                 nc.sync.dma_start(
@@ -174,6 +193,7 @@ def tile_causalselfattention_pa_l_kernel(tc, x, Wk, pk_W, pk_b, out):
         nc.scalar.activation(out=warm_out[:], in_=warm_in[:], func=ACT.Identity)
         for k in range(RAW_BUFS):
             load(k)
+        sort(0)
 
         for k in range(5):
             prep(k)

@@ -14,7 +14,10 @@ ACT = mybir.ActivationFunctionType
 ALU = mybir.AluOpType
 
 P = 128
+SORT = True
 RAW_BUFS = 5
+VEC_BANK = 3
+DEFER = True
 
 
 def tile_causalselfattention_pa_l_kernel(tc, x, Wk, pk_W, pk_b, out):
@@ -29,11 +32,10 @@ def tile_causalselfattention_pa_l_kernel(tc, x, Wk, pk_W, pk_b, out):
         srtp = ctx.enter_context(tc.tile_pool(name="srtp", bufs=2))
         grpp = ctx.enter_context(tc.tile_pool(name="grpp", bufs=4))
         stap = ctx.enter_context(tc.tile_pool(name="stap", bufs=2))
-        khbp = ctx.enter_context(tc.tile_pool(name="khbp", bufs=3))
+        khbp = ctx.enter_context(tc.tile_pool(name="khbp", bufs=6))
         khgp = ctx.enter_context(tc.tile_pool(name="khgp", bufs=3))
         ostp = ctx.enter_context(tc.tile_pool(name="ostp", bufs=3))
-        accp = ctx.enter_context(tc.psum_pool(name="accp", bufs=4))
-        trpp = ctx.enter_context(tc.psum_pool(name="trpp", bufs=4))
+        psum = ctx.enter_context(tc.psum_pool(name="psum", bufs=1))
 
         ident = const.tile([P, P], F32, name="ident")
         make_identity(nc, ident[:])
@@ -53,17 +55,29 @@ def tile_causalselfattention_pa_l_kernel(tc, x, Wk, pk_W, pk_b, out):
                 keep.tile([P, 4, 512], U8, name="khs%d" % j, align_bytes=64),
             )
 
-        halves = [("s", 0, 0), ("w", 0, 0), ("s", 0, 1), ("w", 0, 1)]
-        halves.extend([("w", j, h) for j in range(1, 4) for h in range(2)])
-        halves.extend([("s", s, h) for s in range(1, 16) for h in range(2)])
+        pieces = []
+        for g in range(4):
+            pieces.append(("s", 0, g, 1))
+            pieces.append(("w", 0, g, 1))
+        pieces.extend([("w", j, 2 * h, 2) for j in range(1, 4) for h in range(2)])
+        pieces.extend([("s", s, 2 * h, 2) for s in range(1, 16) for h in range(2)])
 
         raws = {}
         srts = {}
         stationary = {}
-        pending_q = [None]
+        sorted_upto = [-1]
+        rotation = list(range(8))
+        il_todo = []
+        q_todo = []
 
-        def source(kind, idx, h):
-            cols = slice(1024 * h, 1024 * (h + 1))
+        def bank(hold=False):
+            b = rotation.pop(0)
+            if not hold:
+                rotation.append(b)
+            return psum.tile([P, 512], F32, name="bank%d" % b), b
+
+        def source(kind, idx, g0, ng):
+            cols = slice(512 * g0, 512 * (g0 + ng))
             if kind == "w":
                 return Wk[512 * idx : 512 * (idx + 1), cols].rearrange("(a p) k -> p a k", p=P)
             src = xf if (idx // 4) % 2 == 0 else pf
@@ -71,121 +85,164 @@ def tile_causalselfattention_pa_l_kernel(tc, x, Wk, pk_W, pk_b, out):
             return src[r0 : r0 + 512, cols].rearrange("(p a) k -> p a k", a=4)
 
         def load(k):
-            kind, idx, h = halves[k]
-            raw = rawp.tile([P, 4, 1024], BF16, name="raw")
-            nc.sync.dma_start(out=raw[:], in_=source(kind, idx, h))
+            kind, idx, g0, ng = pieces[k]
+            raw = rawp.tile([P, 4, 512 * ng], BF16, name="raw")
+            nc.sync.dma_start(out=raw[:], in_=source(kind, idx, g0, ng))
             raws[k] = raw
 
-        def sort(k):
-            srt = srtp.tile([P, 8, 2, 128], F32, name="srt")
-            nc.vector.tensor_copy(
-                out=srt[:],
-                in_=raws[k][:].bitcast(F32).rearrange("p a (g i u) -> p (a g) u i", g=2, u=2),
-            )
-            srts[k] = srt
-            if k + RAW_BUFS < len(halves):
-                load(k + RAW_BUFS)
+        def sort_upto(k_last):
+            while sorted_upto[0] < min(k_last, len(pieces) - 1):
+                k = sorted_upto[0] + 1
+                sorted_upto[0] = k
+                if SORT:
+                    ng = pieces[k][3]
+                    srt = srtp.tile([P, 4 * ng, 2, 128], F32, name="srt")
+                    nc.vector.tensor_copy(
+                        out=srt[:],
+                        in_=raws[k][:].bitcast(F32).rearrange("p a (g i u) -> p (a g) u i", g=ng, u=2),
+                    )
+                    srts[k] = srt
+                    if k + RAW_BUFS < len(pieces):
+                        load(k + RAW_BUFS)
 
         def prep(k):
-            kind, idx, h = halves[k]
-            if k + 1 < len(halves):
-                sort(k + 1)
+            kind, idx, g0, ng = pieces[k]
             if kind == "w":
                 codes, scales = moving[("w", idx)]
             else:
-                if h == 0:
+                if g0 == 0:
                     stationary[idx] = (
                         stap.tile([P, 4, 512], U32, name="stc", align_bytes=64),
                         stap.tile([P, 4, 512], U8, name="sts", align_bytes=64),
                     )
                 codes, scales = stationary[idx]
-            srt = srts[k]
+            if not SORT:
+                words = raws[k][:].bitcast(F32)
             grouped = []
-            for gl in range(2):
+            for gl in range(ng):
                 grp = grpp.tile([P, 2048], BF16, name="grp", align_bytes=64)
                 grouped.append(grp)
                 gw = grp[:].bitcast(F32)
                 for half in range(2):
-                    tp = trpp.tile([P, 512], F32, name="tp")
+                    tp, b = bank()
                     for a2 in range(2):
                         for u in range(2):
                             q = 2 * a2 + u
-                            nc.tensor.transpose(
-                                tp[:, 128 * q : 128 * (q + 1)],
-                                srt[:, 2 * (2 * half + a2) + gl, u, :],
-                                ident[:],
-                            )
+                            a = 2 * half + a2
+                            if SORT:
+                                in_ = srts[k][:, ng * a + gl, u, :]
+                            else:
+                                in_ = words[:, a, 256 * gl + u : 256 * (gl + 1) : 2]
+                            nc.tensor.transpose(tp[:, 128 * q : 128 * (q + 1)], in_, ident[:])
                     dst = gw[:, 512 * half : 512 * (half + 1)].rearrange("p (a r u) -> p a r u", a=2, u=2)
                     srcv = tp[:].rearrange("p (a u r) -> p a r u", a=2, u=2)
-                    nc.scalar.copy(out=dst, in_=srcv)
-            for gl in range(2):
-                g = 2 * h + gl
+                    if 2 * gl + half == VEC_BANK:
+                        nc.vector.tensor_copy(out=dst, in_=srcv)
+                    else:
+                        nc.scalar.copy(out=dst, in_=srcv)
+            for gl in range(ng):
                 nc.vector.quantize_mx(
-                    out=codes[:, g, :].bitcast(FP8X4),
-                    scales=scales[:, g, :],
+                    out=codes[:, g0 + gl, :].bitcast(FP8X4),
+                    scales=scales[:, g0 + gl, :],
                     in_=grouped[gl][:],
                 )
+            if not SORT and k + RAW_BUFS < len(pieces):
+                load(k + RAW_BUFS)
 
-        def flush_q():
-            if pending_q[0] is not None:
-                khg, j, g = pending_q[0]
-                khc, khs = moving[("k", j)]
-                nc.vector.quantize_mx(
-                    out=khc[:, g, :].bitcast(FP8X4),
-                    scales=khs[:, g, :],
-                    in_=khg[:].rearrange("p c t -> p (c t)"),
-                )
-            pending_q[0] = None
+        def head_prep(k):
+            sort_upto(k + 1)
+            prep(k)
 
-        def unit(s, j):
-            first_stage = (s // 4) % 2 == 0
+        def first_stage(s):
+            return (s // 4) % 2 == 0
+
+        def mm(acc, s, j, t, g):
             stc, sts = stationary[s]
-            mvc, mvs = moving[("w" if first_stage else "k", j)]
-            if first_stage:
-                khb = khbp.tile([P, 4, 512], BF16, name="khb")
-            else:
-                ost = ostp.tile([P, 4, 4, 128], F32, name="ost")
-            for t in range(4):
-                acc = accp.tile([P, 512], F32, name="acc")
-                cols = slice(128 * t, 128 * (t + 1))
-                for g in range(4):
-                    nc.tensor.matmul_mx(
-                        out=acc[:],
-                        lhsT=stc[:, g, cols].bitcast(FP8X4),
-                        lhsT_scale=sts[:, g, cols],
-                        rhs=mvc[:, g, :].bitcast(FP8X4),
-                        rhs_scale=mvs[:, g, :],
-                        start=(g == 0),
-                        stop=(g == 3),
-                    )
-                if first_stage:
-                    nc.scalar.copy(out=khb[:, t, :], in_=acc[:])
-                else:
-                    col = 4 * (4 * (s // 8) + s % 4) + t
-                    accv = acc[:].rearrange("p (h d) -> p h d", h=4)
-                    if t % 2 == 0:
-                        nc.scalar.activation(
-                            out=ost[:, :, t, :], in_=accv, func=ACT.Identity,
-                            bias=bias_f32[:, col : col + 1], scale=1.0,
-                        )
-                    else:
-                        nc.vector.tensor_scalar(
-                            out=ost[:, :, t, :], in0=accv,
-                            scalar1=bias_f32[:, col : col + 1], scalar2=None, op0=ALU.add,
-                        )
-            if first_stage:
-                khg = khgp.tile([P, 512, 4], BF16, name="khg", align_bytes=64)
-                nc.vector.tensor_copy(out=khg[:], in_=khb[:].rearrange("p t c -> p c t"))
-                flush_q()
-                pending_q[0] = (khg, j, s % 4)
-                if s % 4 == 3 and j == 3:
-                    flush_q()
-            else:
-                r0 = 2048 * (s // 8) + 512 * (s % 4)
+            mvc, mvs = moving[("w" if first_stage(s) else "k", j)]
+            cols = slice(128 * t, 128 * (t + 1))
+            nc.tensor.matmul_mx(
+                out=acc[:],
+                lhsT=stc[:, g, cols].bitcast(FP8X4),
+                lhsT_scale=sts[:, g, cols],
+                rhs=mvc[:, g, :].bitcast(FP8X4),
+                rhs_scale=mvs[:, g, :],
+                start=(g == 0),
+                stop=(g == 3),
+            )
+
+        def landing(s):
+            if first_stage(s):
+                return khbp.tile([P, 4, 512], BF16, name="khb")
+            return ostp.tile([P, 4, 4, 128], F32, name="ost")
+
+        def store(s, j, ost, slots):
+            r0 = 2048 * (s // 8) + 512 * (s % 4)
+            rows = out[0, 4 * j : 4 * (j + 1), r0 : r0 + 512, :].rearrange("h (p a) d -> p h a d", a=4)
+            if len(slots) == 4:
                 nc.sync.dma_start(
-                    out=out[0, 4 * j : 4 * (j + 1), r0 : r0 + 512, :].rearrange("h (p a) d -> p h (a d)", a=4),
+                    out=rows.rearrange("p h a d -> p h (a d)"),
                     in_=ost[:].rearrange("p h a d -> p h (a d)"),
                 )
+            else:
+                for t in slots:
+                    nc.sync.dma_start(out=rows[:, :, t, :], in_=ost[:, :, t, :])
+
+        def empty(s, j, t, acc, land):
+            if first_stage(s):
+                nc.scalar.copy(out=land[:, t, :], in_=acc[:])
+                return
+            col = 4 * (4 * (s // 8) + s % 4) + t
+            accv = acc[:].rearrange("p (h d) -> p h d", h=4)
+            if t % 2 == 0:
+                nc.scalar.activation(
+                    out=land[:, :, t, :], in_=accv, func=ACT.Identity,
+                    bias=bias_f32[:, col : col + 1], scale=1.0,
+                )
+            else:
+                nc.vector.tensor_scalar(
+                    out=land[:, :, t, :], in0=accv,
+                    scalar1=bias_f32[:, col : col + 1], scalar2=None, op0=ALU.add,
+                )
+            if s == 15 and j == 3:
+                store(s, j, land, [t])
+
+        def quantise_kh():
+            khg, j, g = q_todo.pop(0)
+            khc, khs = moving[("k", j)]
+            nc.vector.quantize_mx(
+                out=khc[:, g, :].bitcast(FP8X4),
+                scales=khs[:, g, :],
+                in_=khg[:].rearrange("p c t -> p (c t)"),
+            )
+
+        def interleave_kh(count):
+            for i in range(min(count, len(il_todo))):
+                khb, j, g = il_todo.pop(0)
+                khg = khgp.tile([P, 512, 4], BF16, name="khg", align_bytes=64)
+                nc.vector.tensor_copy(out=khg[:], in_=khb[:].rearrange("p t c -> p c t"))
+                if q_todo:
+                    quantise_kh()
+                q_todo.append((khg, j, g))
+
+        def after_unit(s, j, land):
+            if first_stage(s):
+                il_todo.append((land, j, s % 4))
+                if s % 4 == 3 and j == 3:
+                    interleave_kh(len(il_todo))
+                    quantise_kh()
+                elif s > 0 or not DEFER:
+                    interleave_kh(1 + j % 2)
+            elif not (s == 15 and j == 3):
+                store(s, j, land, [0, 1, 2, 3])
+
+        def unit(s, j):
+            land = landing(s)
+            for t in range(4):
+                acc, b = bank()
+                for g in range(4):
+                    mm(acc, s, j, t, g)
+                empty(s, j, t, acc, land)
+            after_unit(s, j, land)
 
         ctx.enter_context(tc.manual_schedule())
 
@@ -193,30 +250,43 @@ def tile_causalselfattention_pa_l_kernel(tc, x, Wk, pk_W, pk_b, out):
         nc.scalar.activation(out=warm_out[:], in_=warm_in[:], func=ACT.Identity)
         for k in range(RAW_BUFS):
             load(k)
-        sort(0)
 
-        for k in range(5):
-            prep(k)
-        unit(0, 0)
-        prep(5)
-        prep(6)
+        for k in range(4):
+            head_prep(k)
+        held = [bank(hold=True) for t in range(4)]
+        land = landing(0)
+        for g in range(4):
+            for t in range(4):
+                mm(held[t][0], 0, 0, t, g)
+                if g == 3:
+                    empty(0, 0, t, held[t][0], land)
+            if g < 2:
+                head_prep(4 + 2 * g)
+                head_prep(5 + 2 * g)
+        rotation.extend([b for acc, b in held])
+        after_unit(0, 0, land)
+        head_prep(8)
+        head_prep(9)
+        head_prep(10)
         unit(0, 1)
-        prep(7)
-        prep(8)
+        head_prep(11)
+        head_prep(12)
         unit(0, 2)
-        prep(9)
-        prep(10)
-        prep(11)
+        head_prep(13)
+        head_prep(14)
+        head_prep(15)
         unit(0, 3)
+        sort_upto(17)
         nc.sync.dma_start(out=bias_raw[:], in_=pk_b.rearrange("c (b p a) -> p (c b) a", p=P, a=4))
         for s in range(1, 16):
-            if s < 15:
-                prep(10 + 2 * s)
             unit(s, 0)
-            unit(s, 1)
             if s < 15:
-                prep(11 + 2 * s)
+                prep(14 + 2 * s)
+                prep(15 + 2 * s)
+            unit(s, 1)
+            sort_upto(16 + 2 * s)
             unit(s, 2)
+            sort_upto(17 + 2 * s)
             unit(s, 3)
             if s == 1:
                 nc.vector.tensor_copy(out=bias_f32[:], in_=bias_raw[:].rearrange("p b a -> p (b a)"))

@@ -59,7 +59,8 @@ def tile_causalselfattention_pa_l_kernel(tc, x, Wk, pk_W, pk_b, out):
         for g in range(4):
             pieces.append(("s", 0, g, 1))
             pieces.append(("w", 0, g, 1))
-        pieces.extend([("w", j, 2 * h, 2) for j in range(1, 4) for h in range(2)])
+        pieces.extend([("w", 1, g, 1) for g in range(4)])
+        pieces.extend([("w", j, 2 * h, 2) for j in range(2, 4) for h in range(2)])
         pieces.extend([("s", s, 2 * h, 2) for s in range(1, 16) for h in range(2)])
 
         raws = {}
@@ -84,7 +85,13 @@ def tile_causalselfattention_pa_l_kernel(tc, x, Wk, pk_W, pk_b, out):
             r0 = 2048 * (idx // 8) + 512 * (idx % 4)
             return src[r0 : r0 + 512, cols].rearrange("(p a) k -> p a k", a=4)
 
-        def load(k):
+        loaded = [0]
+
+        def load_next():
+            k = loaded[0]
+            if k >= len(pieces):
+                return
+            loaded[0] = k + 1
             kind, idx, g0, ng = pieces[k]
             raw = rawp.tile([P, 4, 512 * ng], BF16, name="raw")
             nc.sync.dma_start(out=raw[:], in_=source(kind, idx, g0, ng))
@@ -94,16 +101,15 @@ def tile_causalselfattention_pa_l_kernel(tc, x, Wk, pk_W, pk_b, out):
             while sorted_upto[0] < min(k_last, len(pieces) - 1):
                 k = sorted_upto[0] + 1
                 sorted_upto[0] = k
-                if SORT:
-                    ng = pieces[k][3]
+                ng = pieces[k][3]
+                if ng == 2:
                     srt = srtp.tile([P, 4 * ng, 2, 128], F32, name="srt")
                     nc.vector.tensor_copy(
                         out=srt[:],
                         in_=raws[k][:].bitcast(F32).rearrange("p a (g i u) -> p (a g) u i", g=ng, u=2),
                     )
                     srts[k] = srt
-                    if k + RAW_BUFS < len(pieces):
-                        load(k + RAW_BUFS)
+                    load_next()
 
         def prep(k):
             kind, idx, g0, ng = pieces[k]
@@ -116,7 +122,7 @@ def tile_causalselfattention_pa_l_kernel(tc, x, Wk, pk_W, pk_b, out):
                         stap.tile([P, 4, 512], U8, name="sts", align_bytes=64),
                     )
                 codes, scales = stationary[idx]
-            if not SORT:
+            if ng == 1:
                 words = raws[k][:].bitcast(F32)
             grouped = []
             for gl in range(ng):
@@ -129,14 +135,14 @@ def tile_causalselfattention_pa_l_kernel(tc, x, Wk, pk_W, pk_b, out):
                         for u in range(2):
                             q = 2 * a2 + u
                             a = 2 * half + a2
-                            if SORT:
+                            if ng == 2:
                                 in_ = srts[k][:, ng * a + gl, u, :]
                             else:
                                 in_ = words[:, a, 256 * gl + u : 256 * (gl + 1) : 2]
                             nc.tensor.transpose(tp[:, 128 * q : 128 * (q + 1)], in_, ident[:])
                     dst = gw[:, 512 * half : 512 * (half + 1)].rearrange("p (a r u) -> p a r u", a=2, u=2)
                     srcv = tp[:].rearrange("p (a u r) -> p a r u", a=2, u=2)
-                    if 2 * gl + half == VEC_BANK:
+                    if 2 * gl + half == VEC_BANK or (ng == 1 and half == 1 and kind == "s"):
                         nc.vector.tensor_copy(out=dst, in_=srcv)
                     else:
                         nc.scalar.copy(out=dst, in_=srcv)
@@ -146,8 +152,8 @@ def tile_causalselfattention_pa_l_kernel(tc, x, Wk, pk_W, pk_b, out):
                     scales=scales[:, g0 + gl, :],
                     in_=grouped[gl][:],
                 )
-            if not SORT and k + RAW_BUFS < len(pieces):
-                load(k + RAW_BUFS)
+            if ng == 1:
+                load_next()
 
         def head_prep(k):
             sort_upto(k + 1)
@@ -244,49 +250,50 @@ def tile_causalselfattention_pa_l_kernel(tc, x, Wk, pk_W, pk_b, out):
                 empty(s, j, t, acc, land)
             after_unit(s, j, land)
 
+        def unit_by_pass(s, j, preps):
+            held = [bank(hold=True) for t in range(4)]
+            land = landing(s)
+            for g in range(4):
+                for t in range(4):
+                    mm(held[t][0], s, j, t, g)
+                    if g == 3:
+                        empty(s, j, t, held[t][0], land)
+                for k in preps.get(g, []):
+                    head_prep(k)
+            rotation.extend([b for acc, b in held])
+            after_unit(s, j, land)
+
         ctx.enter_context(tc.manual_schedule())
 
         nc.vector.memset(warm_in[:], 0.0)
         nc.scalar.activation(out=warm_out[:], in_=warm_in[:], func=ACT.Identity)
         for k in range(RAW_BUFS):
-            load(k)
+            load_next()
 
         for k in range(4):
             head_prep(k)
-        held = [bank(hold=True) for t in range(4)]
-        land = landing(0)
-        for g in range(4):
-            for t in range(4):
-                mm(held[t][0], 0, 0, t, g)
-                if g == 3:
-                    empty(0, 0, t, held[t][0], land)
-            if g < 2:
-                head_prep(4 + 2 * g)
-                head_prep(5 + 2 * g)
-        rotation.extend([b for acc, b in held])
-        after_unit(0, 0, land)
-        head_prep(8)
+        unit_by_pass(0, 0, {0: [4, 5], 1: [6, 7], 2: [8]})
         head_prep(9)
         head_prep(10)
-        unit(0, 1)
-        head_prep(11)
-        head_prep(12)
-        unit(0, 2)
+        unit_by_pass(0, 1, {0: [11], 1: [12]})
         head_prep(13)
         head_prep(14)
+        unit(0, 2)
         head_prep(15)
+        head_prep(16)
+        head_prep(17)
         unit(0, 3)
-        sort_upto(17)
+        sort_upto(19)
         nc.sync.dma_start(out=bias_raw[:], in_=pk_b.rearrange("c (b p a) -> p (c b) a", p=P, a=4))
         for s in range(1, 16):
             unit(s, 0)
             if s < 15:
-                prep(14 + 2 * s)
-                prep(15 + 2 * s)
+                prep(16 + 2 * s)
+                prep(17 + 2 * s)
             unit(s, 1)
-            sort_upto(16 + 2 * s)
+            sort_upto(18 + 2 * s)
             unit(s, 2)
-            sort_upto(17 + 2 * s)
+            sort_upto(19 + 2 * s)
             unit(s, 3)
             if s == 1:
                 nc.vector.tensor_copy(out=bias_f32[:], in_=bias_raw[:].rearrange("p b a -> p (b a)"))

from contextlib import ExitStack

import concourse.mybir as mybir
from concourse.masks import make_identity

FLOPS = 2 * 4096 * 2048 * 2048 * 2

F32 = mybir.dt.float32
BF16 = mybir.dt.bfloat16
U32 = mybir.dt.uint32
U8 = mybir.dt.uint8
FP8X4 = mybir.dt.float8_e4m3fn_x4
ACT = mybir.ActivationFunctionType
ALU = mybir.AluOpType

P = 128
SORT = True
RAW_BUFS = 5
VEC_BANK = 3
DEFER = True


def tile_causalselfattention_pa_l_kernel(tc, x, Wk, pk_W, pk_b, out):
    nc = tc.nc
    xf = x.flatten_outer_dims()
    pf = pk_W.flatten_outer_dims()

    with ExitStack() as ctx:
        const = ctx.enter_context(tc.tile_pool(name="const", bufs=1))
        keep = ctx.enter_context(tc.tile_pool(name="keep", bufs=1))
        rawp = ctx.enter_context(tc.tile_pool(name="rawp", bufs=RAW_BUFS))
        srtp = ctx.enter_context(tc.tile_pool(name="srtp", bufs=2))
        grpp = ctx.enter_context(tc.tile_pool(name="grpp", bufs=4))
        stap = ctx.enter_context(tc.tile_pool(name="stap", bufs=2))
        khbp = ctx.enter_context(tc.tile_pool(name="khbp", bufs=6))
        khgp = ctx.enter_context(tc.tile_pool(name="khgp", bufs=3))
        ostp = ctx.enter_context(tc.tile_pool(name="ostp", bufs=3))
        psum = ctx.enter_context(tc.psum_pool(name="psum", bufs=1))

        ident = const.tile([P, P], F32, name="ident")
        make_identity(nc, ident[:])
        warm_in = const.tile([P, 8], F32, name="warm_in")
        warm_out = const.tile([P, 8], F32, name="warm_out")
        bias_raw = const.tile([P, 8, 4], BF16, name="bias_raw")
        bias_f32 = const.tile([P, 32], F32, name="bias_f32")

        moving = {}
        for j in range(4):
            moving[("w", j)] = (
                keep.tile([P, 4, 512], U32, name="wkc%d" % j, align_bytes=64),
                keep.tile([P, 4, 512], U8, name="wks%d" % j, align_bytes=64),
            )
            moving[("k", j)] = (
                keep.tile([P, 4, 512], U32, name="khc%d" % j, align_bytes=64),
                keep.tile([P, 4, 512], U8, name="khs%d" % j, align_bytes=64),
            )

        pieces = []
        for g in range(4):
            pieces.append(("s", 0, g, 1))
            pieces.append(("w", 0, g, 1))
        pieces.extend([("w", 1, g, 1) for g in range(4)])
        pieces.extend([("w", j, 2 * h, 2) for j in range(2, 4) for h in range(2)])
        pieces.extend([("s", s, 2 * h, 2) for s in range(1, 16) for h in range(2)])

        raws = {}
        srts = {}
        stationary = {}
        sorted_upto = [-1]
        rotation = list(range(8))
        il_todo = []
        q_todo = []

        def bank(hold=False):
            b = rotation.pop(0)
            if not hold:
                rotation.append(b)
            return psum.tile([P, 512], F32, name="bank%d" % b), b

        def source(kind, idx, g0, ng):
            cols = slice(512 * g0, 512 * (g0 + ng))
            if kind == "w":
                return Wk[512 * idx : 512 * (idx + 1), cols].rearrange("(a p) k -> p a k", p=P)
            src = xf if (idx // 4) % 2 == 0 else pf
            r0 = 2048 * (idx // 8) + 512 * (idx % 4)
            return src[r0 : r0 + 512, cols].rearrange("(p a) k -> p a k", a=4)

        loaded = [0]

        def load_next():
            k = loaded[0]
            if k >= len(pieces):
                return
            loaded[0] = k + 1
            kind, idx, g0, ng = pieces[k]
            raw = rawp.tile([P, 4, 512 * ng], BF16, name="raw")
            nc.sync.dma_start(out=raw[:], in_=source(kind, idx, g0, ng))
            raws[k] = raw

        def sort_upto(k_last):
            while sorted_upto[0] < min(k_last, len(pieces) - 1):
                k = sorted_upto[0] + 1
                sorted_upto[0] = k
                ng = pieces[k][3]
                if ng == 2:
                    srt = srtp.tile([P, 4 * ng, 2, 128], F32, name="srt")
                    nc.vector.tensor_copy(
                        out=srt[:],
                        in_=raws[k][:].bitcast(F32).rearrange("p a (g i u) -> p (a g) u i", g=ng, u=2),
                    )
                    srts[k] = srt
                    load_next()

        def prep(k):
            kind, idx, g0, ng = pieces[k]
            if kind == "w":
                codes, scales = moving[("w", idx)]
            else:
                if g0 == 0:
                    stationary[idx] = (
                        stap.tile([P, 4, 512], U32, name="stc", align_bytes=64),
                        stap.tile([P, 4, 512], U8, name="sts", align_bytes=64),
                    )
                codes, scales = stationary[idx]
            if ng == 1:
                words = raws[k][:].bitcast(F32)
            grouped = []
            for gl in range(ng):
                grp = grpp.tile([P, 2048], BF16, name="grp", align_bytes=64)
                grouped.append(grp)
                gw = grp[:].bitcast(F32)
                for half in range(2):
                    tp, b = bank()
                    for a2 in range(2):
                        for u in range(2):
                            q = 2 * a2 + u
                            a = 2 * half + a2
                            if ng == 2:
                                in_ = srts[k][:, ng * a + gl, u, :]
                            else:
                                in_ = words[:, a, 256 * gl + u : 256 * (gl + 1) : 2]
                            nc.tensor.transpose(tp[:, 128 * q : 128 * (q + 1)], in_, ident[:])
                    dst = gw[:, 512 * half : 512 * (half + 1)].rearrange("p (a r u) -> p a r u", a=2, u=2)
                    srcv = tp[:].rearrange("p (a u r) -> p a r u", a=2, u=2)
                    if 2 * gl + half == VEC_BANK or (ng == 1 and half == 1 and kind == "s"):
                        nc.vector.tensor_copy(out=dst, in_=srcv)
                    else:
                        nc.scalar.copy(out=dst, in_=srcv)
            for gl in range(ng):
                nc.vector.quantize_mx(
                    out=codes[:, g0 + gl, :].bitcast(FP8X4),
                    scales=scales[:, g0 + gl, :],
                    in_=grouped[gl][:],
                )
            if ng == 1:
                load_next()

        def head_prep(k):
            sort_upto(k + 1)
            prep(k)

        def first_stage(s):
            return (s // 4) % 2 == 0

        def mm(acc, s, j, t, g):
            stc, sts = stationary[s]
            mvc, mvs = moving[("w" if first_stage(s) else "k", j)]
            cols = slice(128 * t, 128 * (t + 1))
            nc.tensor.matmul_mx(
                out=acc[:],
                lhsT=stc[:, g, cols].bitcast(FP8X4),
                lhsT_scale=sts[:, g, cols],
                rhs=mvc[:, g, :].bitcast(FP8X4),
                rhs_scale=mvs[:, g, :],
                start=(g == 0),
                stop=(g == 3),
            )

        def landing(s):
            if first_stage(s):
                return khbp.tile([P, 4, 512], BF16, name="khb")
            return ostp.tile([P, 4, 4, 128], F32, name="ost")

        def store(s, j, ost, slots):
            r0 = 2048 * (s // 8) + 512 * (s % 4)
            rows = out[0, 4 * j : 4 * (j + 1), r0 : r0 + 512, :].rearrange("h (p a) d -> p h a d", a=4)
            if len(slots) == 4:
                nc.sync.dma_start(
                    out=rows.rearrange("p h a d -> p h (a d)"),
                    in_=ost[:].rearrange("p h a d -> p h (a d)"),
                )
            else:
                for t in slots:
                    nc.sync.dma_start(out=rows[:, :, t, :], in_=ost[:, :, t, :])

        def empty(s, j, t, acc, land):
            if first_stage(s):
                nc.scalar.copy(out=land[:, t, :], in_=acc[:])
                return
            col = 4 * (4 * (s // 8) + s % 4) + t
            accv = acc[:].rearrange("p (h d) -> p h d", h=4)
            if t % 2 == 0:
                nc.scalar.activation(
                    out=land[:, :, t, :], in_=accv, func=ACT.Identity,
                    bias=bias_f32[:, col : col + 1], scale=1.0,
                )
            else:
                nc.vector.tensor_scalar(
                    out=land[:, :, t, :], in0=accv,
                    scalar1=bias_f32[:, col : col + 1], scalar2=None, op0=ALU.add,
                )
            if s == 15 and j == 3:
                store(s, j, land, [t])

        def quantise_kh():
            khg, j, g = q_todo.pop(0)
            khc, khs = moving[("k", j)]
            nc.vector.quantize_mx(
                out=khc[:, g, :].bitcast(FP8X4),
                scales=khs[:, g, :],
                in_=khg[:].rearrange("p c t -> p (c t)"),
            )

        def interleave_kh(count):
            for i in range(min(count, len(il_todo))):
                khb, j, g = il_todo.pop(0)
                khg = khgp.tile([P, 512, 4], BF16, name="khg", align_bytes=64)
                nc.vector.tensor_copy(out=khg[:], in_=khb[:].rearrange("p t c -> p c t"))
                if q_todo:
                    quantise_kh()
                q_todo.append((khg, j, g))

        def after_unit(s, j, land):
            if first_stage(s):
                il_todo.append((land, j, s % 4))
                if s % 4 == 3 and j == 3:
                    interleave_kh(len(il_todo))
                    quantise_kh()
                elif s > 0 or not DEFER:
                    interleave_kh(1 + j % 2)
            elif not (s == 15 and j == 3):
                store(s, j, land, [0, 1, 2, 3])

        def unit(s, j):
            land = landing(s)
            for t in range(4):
                acc, b = bank()
                for g in range(4):
                    mm(acc, s, j, t, g)
                empty(s, j, t, acc, land)
            after_unit(s, j, land)

        def unit_by_pass(s, j, preps):
            held = [bank(hold=True) for t in range(4)]
            land = landing(s)
            for g in range(4):
                for t in range(4):
                    mm(held[t][0], s, j, t, g)
                    if g == 3:
                        empty(s, j, t, held[t][0], land)
                for k in preps.get(g, []):
                    head_prep(k)
            rotation.extend([b for acc, b in held])
            after_unit(s, j, land)

        ctx.enter_context(tc.manual_schedule())

        nc.vector.memset(warm_in[:], 0.0)
        nc.scalar.activation(out=warm_out[:], in_=warm_in[:], func=ACT.Identity)
        for k in range(RAW_BUFS):
            load_next()

        for k in range(4):
            head_prep(k)
        unit_by_pass(0, 0, {0: [4, 5], 1: [6, 7], 2: [8]})
        head_prep(9)
        head_prep(10)
        unit_by_pass(0, 1, {0: [11], 1: [12]})
        head_prep(13)
        head_prep(14)
        unit(0, 2)
        head_prep(15)
        head_prep(16)
        head_prep(17)
        unit(0, 3)
        sort_upto(19)
        nc.sync.dma_start(out=bias_raw[:], in_=pk_b.rearrange("c (b p a) -> p (c b) a", p=P, a=4))
        for s in range(1, 16):
            unit(s, 0)
            if s < 15:
                prep(16 + 2 * s)
                prep(17 + 2 * s)
            unit(s, 1)
            sort_upto(18 + 2 * s)
            unit(s, 2)
            sort_upto(19 + 2 * s)
            unit(s, 3)
            if s == 1:
                nc.vector.tensor_copy(out=bias_f32[:], in_=bias_raw[:].rearrange("p b a -> p (b a)"))
